import numpy as np
import ml_dtypes


def mxq(x, axis, fmt="e4m3"):
    dtype, down = {"e4m3": (ml_dtypes.float8_e4m3fn, 7), "e5m2": (ml_dtypes.float8_e5m2, 14)}[fmt]
    v = np.moveaxis(np.asarray(x, np.float32).astype(ml_dtypes.bfloat16).astype(np.float64), axis, -1)
    blocks = v.reshape(v.shape[:-1] + (-1, 32))
    amax = np.abs(blocks).max(-1, keepdims=True)
    byte = np.maximum(np.where(amax > 0, np.frexp(amax)[1] - 1 + 127, 0) - down, 1)
    scale = np.exp2(byte - 127.0)
    codes = (blocks / scale).astype(np.float32).astype(dtype).astype(np.float64)
    return np.moveaxis((codes * scale).reshape(v.shape), -1, axis)


WIDE = False


def mx_kscale(k):
    if not WIDE:
        return np.ones(k)
    levels = np.array([10, -10, 5, -5, 0])
    a = np.random.permutation(np.resize(levels, k // 512 * 4)).reshape(k // 512, 4)
    idx = np.arange(k)
    return np.exp2(a[idx // 512, idx % 128 // 32])


BF16 = ml_dtypes.bfloat16


def bf(x):
    return np.asarray(x, np.float32).astype(BF16)


def f64(x):
    return np.asarray(x).astype(np.float64)


B, N, D, A = 4, 1024, 512, 128
K = D + D
NB = N // A


def setup_inputs():
    st = mx_kscale(K)
    s, t = st[:D], st[D:]
    return {"data": bf(np.random.standard_normal((B, N, D)) * 2.0 * s),
            "pooled": bf(np.random.standard_normal((B, N, A)) * 0.37 / np.sqrt(NB)),
            "W_abs": bf(np.random.standard_normal((A, D)) * 3.0 * np.sqrt(NB / A) * t),
            "W_merge": bf(np.random.standard_normal((K, D)) * 0.5 / np.sqrt(D) / st[:, None])}


def reference(data, pooled, W_abs, W_merge):
    abstract = f64(pooled) @ f64(W_abs)
    x = np.concatenate([f64(data), abstract], axis=-1)
    return mxq(x, 2, "e4m3") @ mxq(f64(W_merge), 0, "e4m3")

@@ -1,0 +1,245 @@
+from contextlib import ExitStack
+
+import concourse.mybir as mybir
+from concourse.masks import make_identity
+
+BF16 = mybir.dt.bfloat16
+F32 = mybir.dt.float32
+U32 = mybir.dt.uint32
+U8 = mybir.dt.uint8
+FP8X4 = mybir.dt.float8_e4m3fn_x4
+
+P = 128
+TOKENS = 4096
+D = 512
+A = 128
+TILES = TOKENS // P
+QUAD = 4
+PAIRS = TILES // 2
+LOOKAHEAD = 4
+QUANT_DELAY = 3
+T_RUNS = {
+    0: (("D", 4), ("D", 5), ("P", 2), ("P", 3)),
+    3: (("D", 6), ("D", 7), ("D", 8), ("D", 9)),
+    7: (("D", 10), ("D", 11), ("D", 12), ("D", 13)),
+    11: (("D", 14), ("D", 15)),
+}
+W_DRAIN = 4
+W_QUANT = 8
+W_REGROUP = 8
+W_PERMUTE = 3
+
+FLOPS = 2 * TOKENS * A * D + 2 * TOKENS * (2 * D) * D
+
+
+def tile_abstraction_pb_kernel(tc, data, pooled, W_abs, W_merge, out):
+    nc = tc.nc
+    data_f = data.flatten_outer_dims().rearrange("(p t) d -> p (t d)", t=TILES)
+    pooled_f = pooled.flatten_outer_dims().rearrange("(p t) a -> p (t a)", t=TILES)
+    out_f = out.flatten_outer_dims().rearrange("(p t) d -> p (t d)", t=TILES)
+
+    with ExitStack() as ctx:
+        keep = ctx.enter_context(tc.tile_pool(name="keep", bufs=1))
+        gx_pool = ctx.enter_context(tc.tile_pool(name="gxp", bufs=5))
+        xq_pool = ctx.enter_context(tc.tile_pool(name="xqp", bufs=5))
+        o_pool = ctx.enter_context(tc.tile_pool(name="op", bufs=6))
+        ring = ctx.enter_context(tc.psum_pool(name="ring", bufs=8))
+        ctx.enter_context(tc.manual_schedule())
+
+        pooled_cuts = ((0, 8), (8, 16), (16, 32))
+        pooled_sb = []
+        for i in range(3):
+            pooled_sb.append(
+                keep.tile([P, (pooled_cuts[i][1] - pooled_cuts[i][0]) * A], BF16, name="pooled%d" % i)
+            )
+        wabs_raw = keep.tile([A, D], BF16, name="wabs_raw")
+        wraw = []
+        for h in range(2):
+            wraw.append(keep.tile([P, 4 * D], BF16, name="wraw%d" % h))
+        data_sb = []
+        for c in range(8):
+            data_sb.append(keep.tile([P, QUAD * D], BF16, name="data%d" % c))
+
+        def load_pooled(i):
+            lo, hi = pooled_cuts[i]
+            nc.sync.dma_start(out=pooled_sb[i][:], in_=pooled_f[:, lo * A : hi * A])
+
+        def load_data(c):
+            nc.sync.dma_start(out=data_sb[c][:], in_=data_f[:, c * QUAD * D : (c + 1) * QUAD * D])
+
+        load_pooled(0)
+        nc.sync.dma_start(out=wabs_raw[:], in_=W_abs)
+        load_pooled(1)
+        nc.sync.dma_start(
+            out=wraw[0][:].rearrange("p (u x) -> p u x", u=2),
+            in_=W_merge[0:D, :].rearrange("(u p e) c -> p u (e c)", u=2, e=2),
+        )
+        nc.sync.dma_start(out=wraw[1][:], in_=W_merge[D : 2 * D, :].rearrange("(p j) c -> p (j c)", j=4))
+        load_data(0)
+        load_data(1)
+        load_pooled(2)
+        for c in range(2, 8):
+            load_data(c)
+
+        ident_b = keep.tile([P, P], BF16, name="ident_b")
+        make_identity(nc, ident_b[:])
+        ident_f = keep.tile([P, P], F32, name="ident_f")
+        make_identity(nc, ident_f[:])
+
+        work = {"v": 0, "s": 0}
+        state = {"fills": 0, "waiting": []}
+
+        def drain(dst, src):
+            if work["v"] <= work["s"]:
+                nc.vector.tensor_copy(out=dst, in_=src)
+                work["v"] += W_DRAIN
+            else:
+                nc.scalar.copy(out=dst, in_=src)
+                work["s"] += W_DRAIN
+
+        gx = {}
+        xq = {}
+        parts = {}
+
+        def grouped(q):
+            if q not in gx:
+                gx[q] = gx_pool.tile([P, 2 * QUAD * D], BF16, name="gx%d" % q, tag="gx", align_bytes=64)
+                parts[q] = 0
+            return gx[q]
+
+        def part_done(q):
+            parts[q] += 1
+            if parts[q] == QUAD + 2:
+                state["waiting"].append((state["fills"] + QUANT_DELAY, q))
+
+        def quantise(q):
+            codes = xq_pool.tile([P, 2 * QUAD * P], U32, name="xc%d" % q, tag="xc", align_bytes=64)
+            scales = xq_pool.tile([P, 2 * QUAD * P], U8, name="xs%d" % q, tag="xs", align_bytes=64)
+            nc.vector.quantize_mx(out=codes[:].bitcast(FP8X4), scales=scales[:], in_=gx[q][:])
+            work["v"] += W_QUANT
+            xq[q] = (codes, scales)
+
+        def after_fill():
+            state["fills"] += 1
+            due = [item for item in state["waiting"] if item[0] <= state["fills"]]
+            state["waiting"] = [item for item in state["waiting"] if item[0] > state["fills"]]
+            for item in due:
+                quantise(item[1])
+
+        pT = []
+        for g in range(4):
+            pT.append(keep.tile([A, 8 * P], BF16, name="pT%d" % g))
+
+        def pooled_T(g):
+            bank = ring.tile([P, 8 * P], BF16, name="bp%d" % g, tag="ring")
+            for k in range(8):
+                t = 8 * g + k
+                i = min(t // 8, 2)
+                off = (t - pooled_cuts[i][0]) * A
+                nc.tensor.transpose(bank[:, k * P : (k + 1) * P], pooled_sb[i][:, off : off + A], ident_b[:])
+            drain(pT[g][:], bank[:])
+            after_fill()
+
+        def data_T(b):
+            q = b // 2
+            bank = ring.tile([P, D], F32, name="bd%d" % b, tag="ring")
+            words = data_sb[q][:].bitcast(F32)
+            for i in range(2):
+                for u in range(2):
+                    col = ((b % 2) * 2 + i) * (D // 2) + u * P
+                    nc.tensor.transpose(
+                        bank[:, (2 * i + u) * P : (2 * i + u + 1) * P], words[:, col : col + P], ident_f[:]
+                    )
+            dst = grouped(q)[:].bitcast(F32)[:, (b % 2) * D : (b % 2 + 1) * D]
+            drain(
+                dst.rearrange("p (i r u) -> p i r u", i=2, u=2),
+                bank[:].rearrange("p (i u r) -> p i r u", i=2, u=2),
+            )
+            part_done(q)
+            after_fill()
+
+        wabs_p = keep.tile([A, D], BF16, name="wabs_p")
+
+        def abstract(t):
+            q = t // QUAD
+            bank = ring.tile([P, D], F32, name="ba%d" % t, tag="ring")
+            for j in range(4):
+                nc.tensor.matmul(
+                    out=bank[:, j * P : (j + 1) * P],
+                    lhsT=wabs_p[:, j * P : (j + 1) * P],
+                    rhs=pT[t // 8][:, (t % 8) * P : (t % 8 + 1) * P],
+                    start=True,
+                    stop=True,
+                )
+            lo = QUAD * D + (t % QUAD) * D
+            drain(
+                grouped(q)[:, lo : lo + D].rearrange("p (r j) -> p r j", j=4),
+                bank[:].rearrange("p (j r) -> p r j", j=4),
+            )
+            part_done(q)
+            after_fill()
+
+        wg = keep.tile([P, 8 * D], BF16, name="wg", align_bytes=64)
+        wc = keep.tile([P, 2 * D], U32, name="wc", align_bytes=64)
+        ws = keep.tile([P, 2 * D], U8, name="ws", align_bytes=64)
+        o_tiles = {}
+
+        def merge(t):
+            q = t // QUAD
+            codes, scales = xq[q]
+            bank = ring.tile([P, D], F32, name="bo%d" % t, tag="ring")
+            for h in range(2):
+                lo = (h * QUAD + t % QUAD) * P
+                nc.tensor.matmul_mx(
+                    out=bank[:],
+                    lhsT=codes[:, lo : lo + P].bitcast(FP8X4),
+                    lhsT_scale=scales[:, lo : lo + P],
+                    rhs=wc[:, h * D : (h + 1) * D].bitcast(FP8X4),
+                    rhs_scale=ws[:, h * D : (h + 1) * D],
+                    start=(h == 0),
+                    stop=(h == 1),
+                )
+            if t % 2 == 0:
+                o_tiles[t // 2] = o_pool.tile([P, 2 * D], F32, name="o%d" % (t // 2), tag="o")
+            o_sb = o_tiles[t // 2]
+            drain(o_sb[:, (t % 2) * D : (t % 2 + 1) * D], bank[:])
+            if t >= TILES - 4:
+                nc.sync.dma_start(out=out_f[:, t * D : (t + 1) * D], in_=o_sb[:, (t % 2) * D : (t % 2 + 1) * D])
+            elif t % 2 == 1:
+                nc.sync.dma_start(out=out_f[:, (t - 1) * D : (t + 1) * D], in_=o_sb[:])
+            after_fill()
+
+        nc.vector.tensor_copy(
+            out=wabs_p[:].rearrange("a (j m) -> a j m", j=4),
+            in_=wabs_raw[:].rearrange("a (m j) -> a j m", j=4),
+        )
+        work["v"] += W_PERMUTE
+        pooled_T(0)
+        pooled_T(1)
+        for h in range(2):
+            nc.vector.tensor_copy(
+                out=wg[:, h * 4 * D : (h + 1) * 4 * D].rearrange("p (c i t) -> p c t i", i=4, t=4),
+                in_=wraw[h][:].rearrange("p (t c i) -> p c t i", t=4, i=4),
+            )
+            work["v"] += W_REGROUP
+        for t in range(6):
+            abstract(t)
+        nc.vector.quantize_mx(out=wc[:].bitcast(FP8X4), scales=ws[:], in_=wg[:])
+        work["v"] += W_QUANT
+        for b in range(4):
+            data_T(b)
+        for t in range(6, 2 * LOOKAHEAD):
+            abstract(t)
+
+        for s in range(PAIRS):
+            for kind, idx in T_RUNS.get(s, ()):
+                if kind == "D":
+                    data_T(idx)
+                else:
+                    pooled_T(idx)
+            ahead = s + LOOKAHEAD
+            if ahead < PAIRS:
+                abstract(2 * ahead)
+                abstract(2 * ahead + 1)
+            merge(2 * s)
+            merge(2 * s + 1)

@@ -15,19 +15,10 @@ D = 512
 A = 128
 TILES = TOKENS // P
 QUAD = 4
-PAIRS = TILES // 2
-LOOKAHEAD = 4
-QUANT_DELAY = 3
-T_RUNS = {
-    0: (("D", 4), ("D", 5), ("P", 2), ("P", 3)),
-    3: (("D", 6), ("D", 7), ("D", 8), ("D", 9)),
-    7: (("D", 10), ("D", 11), ("D", 12), ("D", 13)),
-    11: (("D", 14), ("D", 15)),
-}
-W_DRAIN = 4
-W_QUANT = 8
-W_REGROUP = 8
-W_PERMUTE = 3
+QUADS = TILES // QUAD
+STEPS = TILES // 2
+AHEAD = 4
+T_EVERY = 4
 
 FLOPS = 2 * TOKENS * A * D + 2 * TOKENS * (2 * D) * D
 
@@ -40,32 +31,28 @@ def tile_abstraction_pb_kernel(tc, data, pooled, W_abs, W_merge, out):
 
     with ExitStack() as ctx:
         keep = ctx.enter_context(tc.tile_pool(name="keep", bufs=1))
-        gx_pool = ctx.enter_context(tc.tile_pool(name="gxp", bufs=5))
-        xq_pool = ctx.enter_context(tc.tile_pool(name="xqp", bufs=5))
+        gx_pool = ctx.enter_context(tc.tile_pool(name="gxp", bufs=4))
+        xq_pool = ctx.enter_context(tc.tile_pool(name="xqp", bufs=4))
         o_pool = ctx.enter_context(tc.tile_pool(name="op", bufs=6))
         ring = ctx.enter_context(tc.psum_pool(name="ring", bufs=8))
         ctx.enter_context(tc.manual_schedule())
 
-        pooled_cuts = ((0, 8), (8, 16), (16, 32))
         pooled_sb = []
-        for i in range(3):
-            pooled_sb.append(
-                keep.tile([P, (pooled_cuts[i][1] - pooled_cuts[i][0]) * A], BF16, name="pooled%d" % i)
-            )
+        for g in range(4):
+            pooled_sb.append(keep.tile([P, 8 * A], BF16, name="pooled%d" % g))
         wabs_raw = keep.tile([A, D], BF16, name="wabs_raw")
         wraw = []
         for h in range(2):
             wraw.append(keep.tile([P, 4 * D], BF16, name="wraw%d" % h))
         data_sb = []
-        for c in range(8):
-            data_sb.append(keep.tile([P, QUAD * D], BF16, name="data%d" % c))
+        for q in range(QUADS):
+            data_sb.append(keep.tile([P, QUAD * D], BF16, name="data%d" % q))
 
-        def load_pooled(i):
-            lo, hi = pooled_cuts[i]
-            nc.sync.dma_start(out=pooled_sb[i][:], in_=pooled_f[:, lo * A : hi * A])
+        def load_pooled(g):
+            nc.sync.dma_start(out=pooled_sb[g][:], in_=pooled_f[:, g * 8 * A : (g + 1) * 8 * A])
 
-        def load_data(c):
-            nc.sync.dma_start(out=data_sb[c][:], in_=data_f[:, c * QUAD * D : (c + 1) * QUAD * D])
+        def load_data(q):
+            nc.sync.dma_start(out=data_sb[q][:], in_=data_f[:, q * QUAD * D : (q + 1) * QUAD * D])
 
         load_pooled(0)
         nc.sync.dma_start(out=wabs_raw[:], in_=W_abs)
@@ -78,53 +65,34 @@ def tile_abstraction_pb_kernel(tc, data, pooled, W_abs, W_merge, out):
         load_data(0)
         load_data(1)
         load_pooled(2)
-        for c in range(2, 8):
-            load_data(c)
+        load_pooled(3)
+        for q in range(2, QUADS):
+            load_data(q)
 
         ident_b = keep.tile([P, P], BF16, name="ident_b")
         make_identity(nc, ident_b[:])
         ident_f = keep.tile([P, P], F32, name="ident_f")
         make_identity(nc, ident_f[:])
 
-        work = {"v": 0, "s": 0}
-        state = {"fills": 0, "waiting": []}
-
-        def drain(dst, src):
-            if work["v"] <= work["s"]:
+        def drain(on_vector, dst, src):
+            if on_vector:
                 nc.vector.tensor_copy(out=dst, in_=src)
-                work["v"] += W_DRAIN
             else:
                 nc.scalar.copy(out=dst, in_=src)
-                work["s"] += W_DRAIN
 
         gx = {}
         xq = {}
-        parts = {}
 
         def grouped(q):
             if q not in gx:
                 gx[q] = gx_pool.tile([P, 2 * QUAD * D], BF16, name="gx%d" % q, tag="gx", align_bytes=64)
-                parts[q] = 0
             return gx[q]
-
-        def part_done(q):
-            parts[q] += 1
-            if parts[q] == QUAD + 2:
-                state["waiting"].append((state["fills"] + QUANT_DELAY, q))
 
         def quantise(q):
             codes = xq_pool.tile([P, 2 * QUAD * P], U32, name="xc%d" % q, tag="xc", align_bytes=64)
             scales = xq_pool.tile([P, 2 * QUAD * P], U8, name="xs%d" % q, tag="xs", align_bytes=64)
             nc.vector.quantize_mx(out=codes[:].bitcast(FP8X4), scales=scales[:], in_=gx[q][:])
-            work["v"] += W_QUANT
             xq[q] = (codes, scales)
-
-        def after_fill():
-            state["fills"] += 1
-            due = [item for item in state["waiting"] if item[0] <= state["fills"]]
-            state["waiting"] = [item for item in state["waiting"] if item[0] > state["fills"]]
-            for item in due:
-                quantise(item[1])
 
         pT = []
         for g in range(4):
@@ -133,12 +101,8 @@ def tile_abstraction_pb_kernel(tc, data, pooled, W_abs, W_merge, out):
         def pooled_T(g):
             bank = ring.tile([P, 8 * P], BF16, name="bp%d" % g, tag="ring")
             for k in range(8):
-                t = 8 * g + k
-                i = min(t // 8, 2)
-                off = (t - pooled_cuts[i][0]) * A
-                nc.tensor.transpose(bank[:, k * P : (k + 1) * P], pooled_sb[i][:, off : off + A], ident_b[:])
-            drain(pT[g][:], bank[:])
-            after_fill()
+                nc.tensor.transpose(bank[:, k * P : (k + 1) * P], pooled_sb[g][:, k * A : (k + 1) * A], ident_b[:])
+            drain(False, pT[g][:], bank[:])
 
         def data_T(b):
             q = b // 2
@@ -152,16 +116,14 @@ def tile_abstraction_pb_kernel(tc, data, pooled, W_abs, W_merge, out):
                     )
             dst = grouped(q)[:].bitcast(F32)[:, (b % 2) * D : (b % 2 + 1) * D]
             drain(
+                False,
                 dst.rearrange("p (i r u) -> p i r u", i=2, u=2),
                 bank[:].rearrange("p (i u r) -> p i r u", i=2, u=2),
             )
-            part_done(q)
-            after_fill()
 
         wabs_p = keep.tile([A, D], BF16, name="wabs_p")
 
-        def abstract(t):
-            q = t // QUAD
+        def abstract(t, on_vector):
             bank = ring.tile([P, D], F32, name="ba%d" % t, tag="ring")
             for j in range(4):
                 nc.tensor.matmul(
@@ -173,20 +135,18 @@ def tile_abstraction_pb_kernel(tc, data, pooled, W_abs, W_merge, out):
                 )
             lo = QUAD * D + (t % QUAD) * D
             drain(
-                grouped(q)[:, lo : lo + D].rearrange("p (r j) -> p r j", j=4),
+                on_vector,
+                grouped(t // QUAD)[:, lo : lo + D].rearrange("p (r j) -> p r j", j=4),
                 bank[:].rearrange("p (j r) -> p r j", j=4),
             )
-            part_done(q)
-            after_fill()
 
         wg = keep.tile([P, 8 * D], BF16, name="wg", align_bytes=64)
         wc = keep.tile([P, 2 * D], U32, name="wc", align_bytes=64)
         ws = keep.tile([P, 2 * D], U8, name="ws", align_bytes=64)
         o_tiles = {}
 
-        def merge(t):
-            q = t // QUAD
-            codes, scales = xq[q]
+        def merge(t, on_vector):
+            codes, scales = xq[t // QUAD]
             bank = ring.tile([P, D], F32, name="bo%d" % t, tag="ring")
             for h in range(2):
                 lo = (h * QUAD + t % QUAD) * P
@@ -202,18 +162,16 @@ def tile_abstraction_pb_kernel(tc, data, pooled, W_abs, W_merge, out):
             if t % 2 == 0:
                 o_tiles[t // 2] = o_pool.tile([P, 2 * D], F32, name="o%d" % (t // 2), tag="o")
             o_sb = o_tiles[t // 2]
-            drain(o_sb[:, (t % 2) * D : (t % 2 + 1) * D], bank[:])
-            if t >= TILES - 4:
+            drain(on_vector, o_sb[:, (t % 2) * D : (t % 2 + 1) * D], bank[:])
+            if t >= TILES - QUAD:
                 nc.sync.dma_start(out=out_f[:, t * D : (t + 1) * D], in_=o_sb[:, (t % 2) * D : (t % 2 + 1) * D])
             elif t % 2 == 1:
                 nc.sync.dma_start(out=out_f[:, (t - 1) * D : (t + 1) * D], in_=o_sb[:])
-            after_fill()
 
         nc.vector.tensor_copy(
             out=wabs_p[:].rearrange("a (j m) -> a j m", j=4),
             in_=wabs_raw[:].rearrange("a (m j) -> a j m", j=4),
         )
-        work["v"] += W_PERMUTE
         pooled_T(0)
         pooled_T(1)
         for h in range(2):
@@ -221,25 +179,28 @@ def tile_abstraction_pb_kernel(tc, data, pooled, W_abs, W_merge, out):
                 out=wg[:, h * 4 * D : (h + 1) * 4 * D].rearrange("p (c i t) -> p c t i", i=4, t=4),
                 in_=wraw[h][:].rearrange("p (t c i) -> p c t i", t=4, i=4),
             )
-            work["v"] += W_REGROUP
-        for t in range(6):
-            abstract(t)
+        for t in range(QUAD):
+            abstract(t, t % 2 == 0)
+        data_T(0)
+        data_T(1)
         nc.vector.quantize_mx(out=wc[:].bitcast(FP8X4), scales=ws[:], in_=wg[:])
-        work["v"] += W_QUANT
-        for b in range(4):
-            data_T(b)
-        for t in range(6, 2 * LOOKAHEAD):
-            abstract(t)
+        for t in range(QUAD, 2 * QUAD):
+            abstract(t, t % 2 == 0)
+        quantise(0)
+        data_T(2)
+        data_T(3)
+        pooled_T(2)
+        pooled_T(3)
 
-        for s in range(PAIRS):
-            for kind, idx in T_RUNS.get(s, ()):
-                if kind == "D":
-                    data_T(idx)
-                else:
-                    pooled_T(idx)
-            ahead = s + LOOKAHEAD
-            if ahead < PAIRS:
-                abstract(2 * ahead)
-                abstract(2 * ahead + 1)
-            merge(2 * s)
-            merge(2 * s + 1)
+        for s in range(STEPS):
+            if s % 2 == 0 and s // 2 + 1 < QUADS:
+                quantise(s // 2 + 1)
+            busy = s + AHEAD < STEPS
+            if busy:
+                abstract(2 * (s + AHEAD), True)
+                abstract(2 * (s + AHEAD) + 1, True)
+            if s % T_EVERY == 0 and s + T_EVERY < STEPS:
+                for b in range(s + T_EVERY, s + 2 * T_EVERY):
+                    data_T(b)
+            merge(2 * s, False)
+            merge(2 * s + 1, not busy)

@@ -33,7 +33,7 @@ def tile_abstraction_pb_kernel(tc, data, pooled, W_abs, W_merge, out):
         keep = ctx.enter_context(tc.tile_pool(name="keep", bufs=1))
         gx_pool = ctx.enter_context(tc.tile_pool(name="gxp", bufs=4))
         xq_pool = ctx.enter_context(tc.tile_pool(name="xqp", bufs=4))
-        o_pool = ctx.enter_context(tc.tile_pool(name="op", bufs=6))
+        o_pool = ctx.enter_context(tc.tile_pool(name="op", bufs=10))
         ring = ctx.enter_context(tc.psum_pool(name="ring", bufs=8))
         ctx.enter_context(tc.manual_schedule())
 
@@ -98,13 +98,13 @@ def tile_abstraction_pb_kernel(tc, data, pooled, W_abs, W_merge, out):
         for g in range(4):
             pT.append(keep.tile([A, 8 * P], BF16, name="pT%d" % g))
 
-        def pooled_T(g):
+        def pooled_T(g, on_vector):
             bank = ring.tile([P, 8 * P], BF16, name="bp%d" % g, tag="ring")
             for k in range(8):
                 nc.tensor.transpose(bank[:, k * P : (k + 1) * P], pooled_sb[g][:, k * A : (k + 1) * A], ident_b[:])
-            drain(False, pT[g][:], bank[:])
+            drain(on_vector, pT[g][:], bank[:])
 
-        def data_T(b):
+        def data_T(b, on_vector):
             q = b // 2
             bank = ring.tile([P, D], F32, name="bd%d" % b, tag="ring")
             words = data_sb[q][:].bitcast(F32)
@@ -116,7 +116,7 @@ def tile_abstraction_pb_kernel(tc, data, pooled, W_abs, W_merge, out):
                     )
             dst = grouped(q)[:].bitcast(F32)[:, (b % 2) * D : (b % 2 + 1) * D]
             drain(
-                False,
+                on_vector,
                 dst.rearrange("p (i r u) -> p i r u", i=2, u=2),
                 bank[:].rearrange("p (i u r) -> p i r u", i=2, u=2),
             )
@@ -143,7 +143,6 @@ def tile_abstraction_pb_kernel(tc, data, pooled, W_abs, W_merge, out):
         wg = keep.tile([P, 8 * D], BF16, name="wg", align_bytes=64)
         wc = keep.tile([P, 2 * D], U32, name="wc", align_bytes=64)
         ws = keep.tile([P, 2 * D], U8, name="ws", align_bytes=64)
-        o_tiles = {}
 
         def merge(t, on_vector):
             codes, scales = xq[t // QUAD]
@@ -159,48 +158,44 @@ def tile_abstraction_pb_kernel(tc, data, pooled, W_abs, W_merge, out):
                     start=(h == 0),
                     stop=(h == 1),
                 )
-            if t % 2 == 0:
-                o_tiles[t // 2] = o_pool.tile([P, 2 * D], F32, name="o%d" % (t // 2), tag="o")
-            o_sb = o_tiles[t // 2]
-            drain(on_vector, o_sb[:, (t % 2) * D : (t % 2 + 1) * D], bank[:])
-            if t >= TILES - QUAD:
-                nc.sync.dma_start(out=out_f[:, t * D : (t + 1) * D], in_=o_sb[:, (t % 2) * D : (t % 2 + 1) * D])
-            elif t % 2 == 1:
-                nc.sync.dma_start(out=out_f[:, (t - 1) * D : (t + 1) * D], in_=o_sb[:])
+            o_sb = o_pool.tile([P, D], F32, name="o%d" % t, tag="o")
+            drain(on_vector, o_sb[:], bank[:])
+            nc.sync.dma_start(out=out_f[:, t * D : (t + 1) * D], in_=o_sb[:])
 
         nc.vector.tensor_copy(
             out=wabs_p[:].rearrange("a (j m) -> a j m", j=4),
             in_=wabs_raw[:].rearrange("a (m j) -> a j m", j=4),
         )
-        pooled_T(0)
-        pooled_T(1)
+        pooled_T(0, False)
+        pooled_T(1, False)
         for h in range(2):
             nc.vector.tensor_copy(
                 out=wg[:, h * 4 * D : (h + 1) * 4 * D].rearrange("p (c i t) -> p c t i", i=4, t=4),
                 in_=wraw[h][:].rearrange("p (t c i) -> p c t i", t=4, i=4),
             )
         for t in range(QUAD):
-            abstract(t, t % 2 == 0)
-        data_T(0)
-        data_T(1)
+            abstract(t, False)
+        data_T(0, False)
+        data_T(1, False)
         nc.vector.quantize_mx(out=wc[:].bitcast(FP8X4), scales=ws[:], in_=wg[:])
         for t in range(QUAD, 2 * QUAD):
-            abstract(t, t % 2 == 0)
+            abstract(t, t % 2 == 1)
         quantise(0)
-        data_T(2)
-        data_T(3)
-        pooled_T(2)
-        pooled_T(3)
+        data_T(2, False)
+        data_T(3, True)
+        pooled_T(2, False)
+        pooled_T(3, True)
 
         for s in range(STEPS):
-            if s % 2 == 0 and s // 2 + 1 < QUADS:
+            quantising = s % 2 == 0 and s // 2 + 1 < QUADS
+            if quantising:
                 quantise(s // 2 + 1)
-            busy = s + AHEAD < STEPS
-            if busy:
-                abstract(2 * (s + AHEAD), True)
-                abstract(2 * (s + AHEAD) + 1, True)
+            ahead = s + AHEAD < STEPS
+            if ahead:
+                abstract(2 * (s + AHEAD), False)
+                abstract(2 * (s + AHEAD) + 1, not quantising)
             if s % T_EVERY == 0 and s + T_EVERY < STEPS:
                 for b in range(s + T_EVERY, s + 2 * T_EVERY):
-                    data_T(b)
+                    data_T(b, b % 2 == 1)
             merge(2 * s, False)
-            merge(2 * s + 1, not busy)
+            merge(2 * s + 1, ahead or not quantising)

@@ -18,7 +18,7 @@ QUAD = 4
 QUADS = TILES // QUAD
 STEPS = TILES // 2
 AHEAD = 4
-T_EVERY = 4
+T_EVERY = 2
 
 FLOPS = 2 * TOKENS * A * D + 2 * TOKENS * (2 * D) * D
 
@@ -178,24 +178,29 @@ def tile_abstraction_pb_kernel(tc, data, pooled, W_abs, W_merge, out):
         data_T(0, False)
         data_T(1, False)
         nc.vector.quantize_mx(out=wc[:].bitcast(FP8X4), scales=ws[:], in_=wg[:])
-        for t in range(QUAD, 2 * QUAD):
+        for t in range(QUAD, min(2 * AHEAD, 2 * QUAD)):
             abstract(t, t % 2 == 1)
         quantise(0)
         data_T(2, False)
         data_T(3, True)
         pooled_T(2, False)
         pooled_T(3, True)
+        for t in range(2 * QUAD, 2 * AHEAD):
+            abstract(t, t % 2 == 1)
+        if AHEAD > 4:
+            quantise(1)
 
         for s in range(STEPS):
-            quantising = s % 2 == 0 and s // 2 + 1 < QUADS
+            q_next = (s + AHEAD - 2) // 2
+            quantising = (s + AHEAD) % 2 == 0 and q_next < QUADS and s + AHEAD - 2 >= 2 and (AHEAD <= 4 or q_next >= 2)
             if quantising:
-                quantise(s // 2 + 1)
+                quantise(q_next)
             ahead = s + AHEAD < STEPS
             if ahead:
                 abstract(2 * (s + AHEAD), False)
                 abstract(2 * (s + AHEAD) + 1, not quantising)
-            if s % T_EVERY == 0 and s + T_EVERY < STEPS:
-                for b in range(s + T_EVERY, s + 2 * T_EVERY):
+            if s % T_EVERY == 0 and s + 4 < STEPS:
+                for b in range(s + 4, s + 4 + T_EVERY):
                     data_T(b, b % 2 == 1)
             merge(2 * s, False)
             merge(2 * s + 1, ahead or not quantising)

@@ -16,9 +16,7 @@ A = 128
 TILES = TOKENS // P
 QUAD = 4
 QUADS = TILES // QUAD
-STEPS = TILES // 2
-AHEAD = 4
-T_EVERY = 2
+PAIR = 2 * P
 
 FLOPS = 2 * TOKENS * A * D + 2 * TOKENS * (2 * D) * D
 
@@ -62,10 +60,10 @@ def tile_abstraction_pb_kernel(tc, data, pooled, W_abs, W_merge, out):
             in_=W_merge[0:D, :].rearrange("(u p e) c -> p u (e c)", u=2, e=2),
         )
         nc.sync.dma_start(out=wraw[1][:], in_=W_merge[D : 2 * D, :].rearrange("(p j) c -> p (j c)", j=4))
-        load_data(0)
-        load_data(1)
-        load_pooled(2)
-        load_pooled(3)
+        for q in range(2):
+            load_data(q)
+        for g in range(2, 4):
+            load_pooled(g)
         for q in range(2, QUADS):
             load_data(q)
 
@@ -123,20 +121,20 @@ def tile_abstraction_pb_kernel(tc, data, pooled, W_abs, W_merge, out):
 
         wabs_p = keep.tile([A, D], BF16, name="wabs_p")
 
-        def abstract(t, on_vector):
-            bank = ring.tile([P, D], F32, name="ba%d" % t, tag="ring")
+        def abstract(b, on_vector):
+            bank = ring.tile([P, 4 * PAIR], BF16, name="ba%d" % b, tag="ring")
             for j in range(4):
                 nc.tensor.matmul(
-                    out=bank[:, j * P : (j + 1) * P],
+                    out=bank[:, j * PAIR : (j + 1) * PAIR],
                     lhsT=wabs_p[:, j * P : (j + 1) * P],
-                    rhs=pT[t // 8][:, (t % 8) * P : (t % 8 + 1) * P],
+                    rhs=pT[b // 4][:, (b % 4) * PAIR : (b % 4 + 1) * PAIR],
                     start=True,
                     stop=True,
                 )
-            lo = QUAD * D + (t % QUAD) * D
+            lo = QUAD * D + (b % 2) * 2 * D
             drain(
                 on_vector,
-                grouped(t // QUAD)[:, lo : lo + D].rearrange("p (r j) -> p r j", j=4),
+                grouped(b // 2)[:, lo : lo + 2 * D].rearrange("p (r j) -> p r j", j=4),
                 bank[:].rearrange("p (j r) -> p r j", j=4),
             )
 
@@ -166,41 +164,39 @@ def tile_abstraction_pb_kernel(tc, data, pooled, W_abs, W_merge, out):
             out=wabs_p[:].rearrange("a (j m) -> a j m", j=4),
             in_=wabs_raw[:].rearrange("a (m j) -> a j m", j=4),
         )
-        pooled_T(0, False)
-        pooled_T(1, False)
         for h in range(2):
-            nc.vector.tensor_copy(
-                out=wg[:, h * 4 * D : (h + 1) * 4 * D].rearrange("p (c i t) -> p c t i", i=4, t=4),
-                in_=wraw[h][:].rearrange("p (t c i) -> p c t i", t=4, i=4),
+            nc.gpsimd.tensor_scalar(
+                out=wg[:, h * 4 * D : (h + 1) * 4 * D].rearrange("p (c t) -> p c t", t=4),
+                in0=wraw[h][:].rearrange("p (t c) -> p c t", t=4),
+                scalar1=1.0,
+                scalar2=0.0,
+                op0=mybir.AluOpType.mult,
+                op1=mybir.AluOpType.add,
             )
-        for t in range(QUAD):
-            abstract(t, False)
+        pooled_T(0, False)
+        pooled_T(1, True)
+        abstract(0, False)
+        abstract(1, True)
         data_T(0, False)
-        data_T(1, False)
+        data_T(1, True)
+        abstract(2, False)
         nc.vector.quantize_mx(out=wc[:].bitcast(FP8X4), scales=ws[:], in_=wg[:])
-        for t in range(QUAD, min(2 * AHEAD, 2 * QUAD)):
-            abstract(t, t % 2 == 1)
+        pooled_T(2, False)
         quantise(0)
         data_T(2, False)
+        abstract(3, False)
         data_T(3, True)
-        pooled_T(2, False)
         pooled_T(3, True)
-        for t in range(2 * QUAD, 2 * AHEAD):
-            abstract(t, t % 2 == 1)
-        if AHEAD > 4:
-            quantise(1)
 
-        for s in range(STEPS):
-            q_next = (s + AHEAD - 2) // 2
-            quantising = (s + AHEAD) % 2 == 0 and q_next < QUADS and s + AHEAD - 2 >= 2 and (AHEAD <= 4 or q_next >= 2)
-            if quantising:
-                quantise(q_next)
-            ahead = s + AHEAD < STEPS
-            if ahead:
-                abstract(2 * (s + AHEAD), False)
-                abstract(2 * (s + AHEAD) + 1, not quantising)
-            if s % T_EVERY == 0 and s + 4 < STEPS:
-                for b in range(s + 4, s + 4 + T_EVERY):
-                    data_T(b, b % 2 == 1)
-            merge(2 * s, False)
-            merge(2 * s + 1, ahead or not quantising)
+        for q in range(QUADS):
+            if q + 1 < QUADS:
+                quantise(q + 1)
+            filling = q + 2 < QUADS
+            if filling:
+                data_T(2 * q + 4, True)
+                data_T(2 * q + 5, True)
+            for half in range(2):
+                if filling:
+                    abstract(2 * q + 4 + half, False)
+                merge(QUAD * q + 2 * half, False)
+                merge(QUAD * q + 2 * half + 1, True)

@@ -16,6 +16,7 @@ A = 128
 TILES = TOKENS // P
 QUAD = 4
 QUADS = TILES // QUAD
+WARM_HEAD = 5
 PAIR = 2 * P
 
 FLOPS = 2 * TOKENS * A * D + 2 * TOKENS * (2 * D) * D
@@ -67,6 +68,8 @@ def tile_abstraction_pb_kernel(tc, data, pooled, W_abs, W_merge, out):
         for q in range(2, QUADS):
             load_data(q)
 
+        idle = keep.tile([P, D], BF16, name="idle")
+        nc.vector.memset(idle[:], 0.0)
         ident_b = keep.tile([P, P], BF16, name="ident_b")
         make_identity(nc, ident_b[:])
         ident_f = keep.tile([P, P], F32, name="ident_f")
@@ -118,6 +121,14 @@ def tile_abstraction_pb_kernel(tc, data, pooled, W_abs, W_merge, out):
                 dst.rearrange("p (i r u) -> p i r u", i=2, u=2),
                 bank[:].rearrange("p (i u r) -> p i r u", i=2, u=2),
             )
+
+        warm = [0]
+
+        def warm_up(n):
+            bank = ring.tile([P, D], F32, name="bw%d" % warm[0], tag="ring")
+            warm[0] += 1
+            for k in range(n):
+                nc.tensor.matmul(out=bank[:], lhsT=idle[:, 0:P], rhs=idle[:], start=True, stop=True)
 
         wabs_p = keep.tile([A, D], BF16, name="wabs_p")
 
@@ -173,18 +184,22 @@ def tile_abstraction_pb_kernel(tc, data, pooled, W_abs, W_merge, out):
                 op0=mybir.AluOpType.mult,
                 op1=mybir.AluOpType.add,
             )
+        warm_up(WARM_HEAD)
         pooled_T(0, False)
         pooled_T(1, True)
+        warm_up(2)
         abstract(0, False)
         abstract(1, True)
         data_T(0, False)
         data_T(1, True)
         abstract(2, False)
         nc.vector.quantize_mx(out=wc[:].bitcast(FP8X4), scales=ws[:], in_=wg[:])
+        warm_up(2)
         pooled_T(2, False)
         quantise(0)
         data_T(2, False)
         abstract(3, False)
+        warm_up(2)
         data_T(3, True)
         pooled_T(3, True)
 

@@ -30,7 +30,7 @@ def tile_abstraction_pb_kernel(tc, data, pooled, W_abs, W_merge, out):
 
     with ExitStack() as ctx:
         keep = ctx.enter_context(tc.tile_pool(name="keep", bufs=1))
-        gx_pool = ctx.enter_context(tc.tile_pool(name="gxp", bufs=4))
+        gx_pool = ctx.enter_context(tc.tile_pool(name="gxp", bufs=5))
         xq_pool = ctx.enter_context(tc.tile_pool(name="xqp", bufs=4))
         o_pool = ctx.enter_context(tc.tile_pool(name="op", bufs=10))
         ring = ctx.enter_context(tc.psum_pool(name="ring", bufs=8))
@@ -55,17 +55,18 @@ def tile_abstraction_pb_kernel(tc, data, pooled, W_abs, W_merge, out):
 
         load_pooled(0)
         nc.sync.dma_start(out=wabs_raw[:], in_=W_abs)
-        load_pooled(1)
         nc.sync.dma_start(
             out=wraw[0][:].rearrange("p (u x) -> p u x", u=2),
             in_=W_merge[0:D, :].rearrange("(u p e) c -> p u (e c)", u=2, e=2),
         )
+        load_pooled(1)
+        load_data(0)
         nc.sync.dma_start(out=wraw[1][:], in_=W_merge[D : 2 * D, :].rearrange("(p j) c -> p (j c)", j=4))
-        for q in range(2):
-            load_data(q)
-        for g in range(2, 4):
-            load_pooled(g)
-        for q in range(2, QUADS):
+        load_data(1)
+        load_pooled(2)
+        load_data(2)
+        load_pooled(3)
+        for q in range(3, QUADS):
             load_data(q)
 
         idle = keep.tile([P, D], BF16, name="idle")
@@ -175,43 +176,52 @@ def tile_abstraction_pb_kernel(tc, data, pooled, W_abs, W_merge, out):
             out=wabs_p[:].rearrange("a (j m) -> a j m", j=4),
             in_=wabs_raw[:].rearrange("a (m j) -> a j m", j=4),
         )
-        for h in range(2):
-            nc.gpsimd.tensor_scalar(
-                out=wg[:, h * 4 * D : (h + 1) * 4 * D].rearrange("p (c t) -> p c t", t=4),
-                in0=wraw[h][:].rearrange("p (t c) -> p c t", t=4),
-                scalar1=1.0,
-                scalar2=0.0,
-                op0=mybir.AluOpType.mult,
-                op1=mybir.AluOpType.add,
+
+        def group_w(h):
+            nc.vector.tensor_copy(
+                out=wg[:, h * 4 * D : (h + 1) * 4 * D].rearrange("p (c i t) -> p c t i", i=4, t=4),
+                in_=wraw[h][:].rearrange("p (t c i) -> p c t i", t=4, i=4),
             )
+
+        def quantise_w(h):
+            nc.vector.quantize_mx(
+                out=wc[:, h * D : (h + 1) * D].bitcast(FP8X4),
+                scales=ws[:, h * D : (h + 1) * D],
+                in_=wg[:, h * 4 * D : (h + 1) * 4 * D],
+            )
+
         warm_up(WARM_HEAD)
         pooled_T(0, False)
-        pooled_T(1, True)
-        warm_up(2)
+        group_w(0)
         abstract(0, False)
         abstract(1, True)
+        pooled_T(1, False)
         data_T(0, False)
-        data_T(1, True)
+        data_T(1, False)
+        group_w(1)
         abstract(2, False)
-        nc.vector.quantize_mx(out=wc[:].bitcast(FP8X4), scales=ws[:], in_=wg[:])
-        warm_up(2)
-        pooled_T(2, False)
-        quantise(0)
+        quantise_w(0)
+        abstract(3, True)
         data_T(2, False)
-        abstract(3, False)
-        warm_up(2)
-        data_T(3, True)
+        quantise(0)
+        quantise_w(1)
+        data_T(3, False)
+        pooled_T(2, True)
+        abstract(4, False)
+        data_T(4, True)
+        data_T(5, False)
+        abstract(5, False)
         pooled_T(3, True)
 
         for q in range(QUADS):
             if q + 1 < QUADS:
                 quantise(q + 1)
-            filling = q + 2 < QUADS
+            filling = q + 3 < QUADS
             if filling:
-                data_T(2 * q + 4, True)
-                data_T(2 * q + 5, True)
+                data_T(2 * q + 6, True)
+                data_T(2 * q + 7, True)
             for half in range(2):
                 if filling:
-                    abstract(2 * q + 4 + half, False)
+                    abstract(2 * q + 6 + half, False)
                 merge(QUAD * q + 2 * half, False)
                 merge(QUAD * q + 2 * half + 1, True)

@@ -55,11 +55,11 @@ def tile_abstraction_pb_kernel(tc, data, pooled, W_abs, W_merge, out):
 
         load_pooled(0)
         nc.sync.dma_start(out=wabs_raw[:], in_=W_abs)
+        load_pooled(1)
         nc.sync.dma_start(
             out=wraw[0][:].rearrange("p (u x) -> p u x", u=2),
             in_=W_merge[0:D, :].rearrange("(u p e) c -> p u (e c)", u=2, e=2),
         )
-        load_pooled(1)
         load_data(0)
         nc.sync.dma_start(out=wraw[1][:], in_=W_merge[D : 2 * D, :].rearrange("(p j) c -> p (j c)", j=4))
         load_data(1)
@@ -192,16 +192,16 @@ def tile_abstraction_pb_kernel(tc, data, pooled, W_abs, W_merge, out):
 
         warm_up(WARM_HEAD)
         pooled_T(0, False)
-        group_w(0)
+        pooled_T(1, True)
         abstract(0, False)
+        group_w(0)
         abstract(1, True)
-        pooled_T(1, False)
-        data_T(0, False)
+        abstract(2, False)
+        data_T(0, True)
         data_T(1, False)
         group_w(1)
-        abstract(2, False)
         quantise_w(0)
-        abstract(3, True)
+        abstract(3, False)
         data_T(2, False)
         quantise(0)
         quantise_w(1)
@@ -216,12 +216,13 @@ def tile_abstraction_pb_kernel(tc, data, pooled, W_abs, W_merge, out):
         for q in range(QUADS):
             if q + 1 < QUADS:
                 quantise(q + 1)
-            filling = q + 3 < QUADS
+            fill = q + 3 if q < 2 else (QUADS if q == 2 else q + 2)
+            filling = fill < QUADS
             if filling:
-                data_T(2 * q + 6, True)
-                data_T(2 * q + 7, True)
+                data_T(2 * fill, True)
+                data_T(2 * fill + 1, True)
             for half in range(2):
                 if filling:
-                    abstract(2 * q + 6 + half, False)
+                    abstract(2 * fill + half, False)
                 merge(QUAD * q + 2 * half, False)
                 merge(QUAD * q + 2 * half + 1, True)

@@ -16,6 +16,7 @@ A = 128
 TILES = TOKENS // P
 QUAD = 4
 QUADS = TILES // QUAD
+PAIRS = TILES // 2
 WARM_HEAD = 5
 PAIR = 2 * P
 
@@ -30,7 +31,7 @@ def tile_abstraction_pb_kernel(tc, data, pooled, W_abs, W_merge, out):
 
     with ExitStack() as ctx:
         keep = ctx.enter_context(tc.tile_pool(name="keep", bufs=1))
-        gx_pool = ctx.enter_context(tc.tile_pool(name="gxp", bufs=5))
+        gx_pool = ctx.enter_context(tc.tile_pool(name="gxp", bufs=8))
         xq_pool = ctx.enter_context(tc.tile_pool(name="xqp", bufs=4))
         o_pool = ctx.enter_context(tc.tile_pool(name="op", bufs=10))
         ring = ctx.enter_context(tc.psum_pool(name="ring", bufs=8))
@@ -85,16 +86,16 @@ def tile_abstraction_pb_kernel(tc, data, pooled, W_abs, W_merge, out):
         gx = {}
         xq = {}
 
-        def grouped(q):
-            if q not in gx:
-                gx[q] = gx_pool.tile([P, 2 * QUAD * D], BF16, name="gx%d" % q, tag="gx", align_bytes=64)
-            return gx[q]
+        def grouped(b):
+            if b not in gx:
+                gx[b] = gx_pool.tile([P, 4 * D], BF16, name="gx%d" % b, tag="gx", align_bytes=64)
+            return gx[b]
 
-        def quantise(q):
-            codes = xq_pool.tile([P, 2 * QUAD * P], U32, name="xc%d" % q, tag="xc", align_bytes=64)
-            scales = xq_pool.tile([P, 2 * QUAD * P], U8, name="xs%d" % q, tag="xs", align_bytes=64)
-            nc.vector.quantize_mx(out=codes[:].bitcast(FP8X4), scales=scales[:], in_=gx[q][:])
-            xq[q] = (codes, scales)
+        def quantise(b):
+            codes = xq_pool.tile([P, 4 * P], U32, name="xc%d" % b, tag="xc", align_bytes=64)
+            scales = xq_pool.tile([P, 4 * P], U8, name="xs%d" % b, tag="xs", align_bytes=64)
+            nc.vector.quantize_mx(out=codes[:].bitcast(FP8X4), scales=scales[:], in_=gx[b][:])
+            xq[b] = (codes, scales)
 
         pT = []
         for g in range(4):
@@ -116,7 +117,7 @@ def tile_abstraction_pb_kernel(tc, data, pooled, W_abs, W_merge, out):
                     nc.tensor.transpose(
                         bank[:, (2 * i + u) * P : (2 * i + u + 1) * P], words[:, col : col + P], ident_f[:]
                     )
-            dst = grouped(q)[:].bitcast(F32)[:, (b % 2) * D : (b % 2 + 1) * D]
+            dst = grouped(b)[:].bitcast(F32)[:, 0:D]
             drain(
                 on_vector,
                 dst.rearrange("p (i r u) -> p i r u", i=2, u=2),
@@ -143,10 +144,9 @@ def tile_abstraction_pb_kernel(tc, data, pooled, W_abs, W_merge, out):
                     start=True,
                     stop=True,
                 )
-            lo = QUAD * D + (b % 2) * 2 * D
             drain(
                 on_vector,
-                grouped(b // 2)[:, lo : lo + 2 * D].rearrange("p (r j) -> p r j", j=4),
+                grouped(b)[:, 2 * D : 4 * D].rearrange("p (r j) -> p r j", j=4),
                 bank[:].rearrange("p (j r) -> p r j", j=4),
             )
 
@@ -155,10 +155,10 @@ def tile_abstraction_pb_kernel(tc, data, pooled, W_abs, W_merge, out):
         ws = keep.tile([P, 2 * D], U8, name="ws", align_bytes=64)
 
         def merge(t, on_vector):
-            codes, scales = xq[t // QUAD]
+            codes, scales = xq[t // 2]
             bank = ring.tile([P, D], F32, name="bo%d" % t, tag="ring")
             for h in range(2):
-                lo = (h * QUAD + t % QUAD) * P
+                lo = (h * 2 + t % 2) * P
                 nc.tensor.matmul_mx(
                     out=bank[:],
                     lhsT=codes[:, lo : lo + P].bitcast(FP8X4),
@@ -202,27 +202,28 @@ def tile_abstraction_pb_kernel(tc, data, pooled, W_abs, W_merge, out):
         group_w(1)
         quantise_w(0)
         abstract(3, False)
-        data_T(2, False)
+        data_T(2, True)
+        data_T(3, False)
+        pooled_T(2, False)
         quantise(0)
         quantise_w(1)
-        data_T(3, False)
-        pooled_T(2, True)
         abstract(4, False)
         data_T(4, True)
         data_T(5, False)
-        abstract(5, False)
         pooled_T(3, True)
+        quantise(1)
+        abstract(5, False)
 
         for q in range(QUADS):
-            if q + 1 < QUADS:
-                quantise(q + 1)
-            fill = q + 3 if q < 2 else (QUADS if q == 2 else q + 2)
+            fill = q + 3 - q // 3 if q % 3 != 2 else QUADS
             filling = fill < QUADS
             if filling:
+                abstract(2 * fill, False)
                 data_T(2 * fill, True)
                 data_T(2 * fill + 1, True)
+                abstract(2 * fill + 1, False)
             for half in range(2):
-                if filling:
-                    abstract(2 * fill + half, False)
+                if q + 1 < QUADS:
+                    quantise(2 * q + 2 + half)
                 merge(QUAD * q + 2 * half, False)
                 merge(QUAD * q + 2 * half + 1, True)

@@ -56,11 +56,11 @@ def tile_abstraction_pb_kernel(tc, data, pooled, W_abs, W_merge, out):
 
         load_pooled(0)
         nc.sync.dma_start(out=wabs_raw[:], in_=W_abs)
-        load_pooled(1)
         nc.sync.dma_start(
             out=wraw[0][:].rearrange("p (u x) -> p u x", u=2),
             in_=W_merge[0:D, :].rearrange("(u p e) c -> p u (e c)", u=2, e=2),
         )
+        load_pooled(1)
         load_data(0)
         nc.sync.dma_start(out=wraw[1][:], in_=W_merge[D : 2 * D, :].rearrange("(p j) c -> p (j c)", j=4))
         load_data(1)
@@ -192,27 +192,27 @@ def tile_abstraction_pb_kernel(tc, data, pooled, W_abs, W_merge, out):
 
         warm_up(WARM_HEAD)
         pooled_T(0, False)
-        pooled_T(1, True)
-        abstract(0, False)
         group_w(0)
+        abstract(0, False)
         abstract(1, True)
-        abstract(2, False)
-        data_T(0, True)
+        pooled_T(1, False)
+        data_T(0, False)
         data_T(1, False)
         group_w(1)
+        abstract(2, False)
         quantise_w(0)
-        abstract(3, False)
-        data_T(2, True)
-        data_T(3, False)
-        pooled_T(2, False)
+        abstract(3, True)
+        data_T(2, False)
         quantise(0)
         quantise_w(1)
+        data_T(3, False)
+        pooled_T(2, True)
         abstract(4, False)
         data_T(4, True)
         data_T(5, False)
-        pooled_T(3, True)
         quantise(1)
         abstract(5, False)
+        pooled_T(3, True)
 
         for q in range(QUADS):
             fill = q + 3 - q // 3 if q % 3 != 2 else QUADS

@@ -17,7 +17,6 @@ TILES = TOKENS // P
 QUAD = 4
 QUADS = TILES // QUAD
 PAIRS = TILES // 2
-WARM_HEAD = 5
 PAIR = 2 * P
 
 FLOPS = 2 * TOKENS * A * D + 2 * TOKENS * (2 * D) * D
@@ -190,9 +189,10 @@ def tile_abstraction_pb_kernel(tc, data, pooled, W_abs, W_merge, out):
                 in_=wg[:, h * 4 * D : (h + 1) * 4 * D],
             )
 
-        warm_up(WARM_HEAD)
+        warm_up(2)
         pooled_T(0, False)
         group_w(0)
+        warm_up(2)
         abstract(0, False)
         abstract(1, True)
         pooled_T(1, False)

@@ -53,7 +53,10 @@ def tile_abstraction_pb_kernel(tc, data, pooled, W_abs, W_merge, out):
         def load_data(q):
             nc.sync.dma_start(out=data_sb[q][:], in_=data_f[:, q * QUAD * D : (q + 1) * QUAD * D])
 
-        load_pooled(0)
+        for k in range(2):
+            nc.sync.dma_start(
+                out=pooled_sb[0][:, k * 4 * A : (k + 1) * 4 * A], in_=pooled_f[:, k * 4 * A : (k + 1) * 4 * A]
+            )
         nc.sync.dma_start(out=wabs_raw[:], in_=W_abs)
         nc.sync.dma_start(
             out=wraw[0][:].rearrange("p (u x) -> p u x", u=2),
@@ -62,9 +65,9 @@ def tile_abstraction_pb_kernel(tc, data, pooled, W_abs, W_merge, out):
         load_pooled(1)
         load_data(0)
         nc.sync.dma_start(out=wraw[1][:], in_=W_merge[D : 2 * D, :].rearrange("(p j) c -> p (j c)", j=4))
-        load_data(1)
         load_pooled(2)
-        load_data(2)
+        for q in range(1, 3):
+            load_data(q)
         load_pooled(3)
         for q in range(3, QUADS):
             load_data(q)
@@ -100,11 +103,13 @@ def tile_abstraction_pb_kernel(tc, data, pooled, W_abs, W_merge, out):
         for g in range(4):
             pT.append(keep.tile([A, 8 * P], BF16, name="pT%d" % g))
 
-        def pooled_T(g, on_vector):
-            bank = ring.tile([P, 8 * P], BF16, name="bp%d" % g, tag="ring")
-            for k in range(8):
-                nc.tensor.transpose(bank[:, k * P : (k + 1) * P], pooled_sb[g][:, k * A : (k + 1) * A], ident_b[:])
-            drain(on_vector, pT[g][:], bank[:])
+        def pooled_T(g, on_vector, first=0, tiles=8):
+            bank = ring.tile([P, tiles * P], BF16, name="bp%d_%d" % (g, first), tag="ring")
+            for k in range(tiles):
+                nc.tensor.transpose(
+                    bank[:, k * P : (k + 1) * P], pooled_sb[g][:, (first + k) * A : (first + k + 1) * A], ident_b[:]
+                )
+            drain(on_vector, pT[g][:, first * P : (first + tiles) * P], bank[:])
 
         def data_T(b, on_vector):
             q = b // 2
@@ -190,28 +195,29 @@ def tile_abstraction_pb_kernel(tc, data, pooled, W_abs, W_merge, out):
             )
 
         warm_up(2)
-        pooled_T(0, False)
+        pooled_T(0, False, 0, 4)
+        pooled_T(0, False, 4, 4)
         group_w(0)
         warm_up(2)
         abstract(0, False)
-        abstract(1, True)
         pooled_T(1, False)
-        data_T(0, False)
-        data_T(1, False)
-        group_w(1)
+        abstract(1, True)
         abstract(2, False)
+        group_w(1)
+        data_T(0, False)
+        data_T(1, True)
+        abstract(3, False)
         quantise_w(0)
-        abstract(3, True)
-        data_T(2, False)
-        quantise(0)
-        quantise_w(1)
-        data_T(3, False)
         pooled_T(2, True)
+        quantise(0)
         abstract(4, False)
-        data_T(4, True)
-        data_T(5, False)
+        quantise_w(1)
+        data_T(2, True)
+        data_T(3, False)
         quantise(1)
         abstract(5, False)
+        data_T(4, True)
+        data_T(5, False)
         pooled_T(3, True)
 
         for q in range(QUADS):

@@ -17,6 +17,7 @@ TILES = TOKENS // P
 QUAD = 4
 QUADS = TILES // QUAD
 PAIRS = TILES // 2
+LAST = TILES - 2
 PAIR = 2 * P
 
 FLOPS = 2 * TOKENS * A * D + 2 * TOKENS * (2 * D) * D
@@ -32,7 +33,7 @@ def tile_abstraction_pb_kernel(tc, data, pooled, W_abs, W_merge, out):
         keep = ctx.enter_context(tc.tile_pool(name="keep", bufs=1))
         gx_pool = ctx.enter_context(tc.tile_pool(name="gxp", bufs=8))
         xq_pool = ctx.enter_context(tc.tile_pool(name="xqp", bufs=4))
-        o_pool = ctx.enter_context(tc.tile_pool(name="op", bufs=10))
+        o_pool = ctx.enter_context(tc.tile_pool(name="op", bufs=6))
         ring = ctx.enter_context(tc.psum_pool(name="ring", bufs=8))
         ctx.enter_context(tc.manual_schedule())
 
@@ -158,6 +159,8 @@ def tile_abstraction_pb_kernel(tc, data, pooled, W_abs, W_merge, out):
         wc = keep.tile([P, 2 * D], U32, name="wc", align_bytes=64)
         ws = keep.tile([P, 2 * D], U8, name="ws", align_bytes=64)
 
+        o_pair = {}
+
         def merge(t, on_vector):
             codes, scales = xq[t // 2]
             bank = ring.tile([P, D], F32, name="bo%d" % t, tag="ring")
@@ -172,9 +175,14 @@ def tile_abstraction_pb_kernel(tc, data, pooled, W_abs, W_merge, out):
                     start=(h == 0),
                     stop=(h == 1),
                 )
-            o_sb = o_pool.tile([P, D], F32, name="o%d" % t, tag="o")
-            drain(on_vector, o_sb[:], bank[:])
-            nc.sync.dma_start(out=out_f[:, t * D : (t + 1) * D], in_=o_sb[:])
+            if t % 2 == 0:
+                o_pair[t // 2] = o_pool.tile([P, 2 * D], F32, name="o%d" % t, tag="o")
+            o_sb = o_pair[t // 2]
+            drain(on_vector, o_sb[:, (t % 2) * D : (t % 2 + 1) * D], bank[:])
+            if t >= LAST:
+                nc.sync.dma_start(out=out_f[:, t * D : (t + 1) * D], in_=o_sb[:, (t % 2) * D : (t % 2 + 1) * D])
+            elif t % 2 == 1:
+                nc.sync.dma_start(out=out_f[:, (t - 1) * D : (t + 1) * D], in_=o_sb[:])
 
         nc.vector.tensor_copy(
             out=wabs_p[:].rearrange("a (j m) -> a j m", j=4),

from contextlib import ExitStack

import concourse.mybir as mybir
from concourse.masks import make_identity

BF16 = mybir.dt.bfloat16
F32 = mybir.dt.float32
U32 = mybir.dt.uint32
U8 = mybir.dt.uint8
FP8X4 = mybir.dt.float8_e4m3fn_x4

P = 128
TOKENS = 4096
D = 512
A = 128
TILES = TOKENS // P
QUAD = 4
QUADS = TILES // QUAD
PAIRS = TILES // 2
LAST = TILES - 2
PAIR = 2 * P

FLOPS = 2 * TOKENS * A * D + 2 * TOKENS * (2 * D) * D


def tile_abstraction_pb_kernel(tc, data, pooled, W_abs, W_merge, out):
    nc = tc.nc
    data_f = data.flatten_outer_dims().rearrange("(p t) d -> p (t d)", t=TILES)
    pooled_f = pooled.flatten_outer_dims().rearrange("(p t) a -> p (t a)", t=TILES)
    out_f = out.flatten_outer_dims().rearrange("(p t) d -> p (t d)", t=TILES)

    with ExitStack() as ctx:
        keep = ctx.enter_context(tc.tile_pool(name="keep", bufs=1))
        gx_pool = ctx.enter_context(tc.tile_pool(name="gxp", bufs=8))
        xq_pool = ctx.enter_context(tc.tile_pool(name="xqp", bufs=4))
        o_pool = ctx.enter_context(tc.tile_pool(name="op", bufs=6))
        ring = ctx.enter_context(tc.psum_pool(name="ring", bufs=8))
        ctx.enter_context(tc.manual_schedule())

        pooled_sb = []
        for g in range(4):
            pooled_sb.append(keep.tile([P, 8 * A], BF16, name="pooled%d" % g))
        wabs_raw = keep.tile([A, D], BF16, name="wabs_raw")
        wraw = []
        for h in range(2):
            wraw.append(keep.tile([P, 4 * D], BF16, name="wraw%d" % h))
        data_sb = []
        for q in range(QUADS):
            data_sb.append(keep.tile([P, QUAD * D], BF16, name="data%d" % q))

        def load_pooled(g):
            nc.sync.dma_start(out=pooled_sb[g][:], in_=pooled_f[:, g * 8 * A : (g + 1) * 8 * A])

        def load_data(q):
            nc.sync.dma_start(out=data_sb[q][:], in_=data_f[:, q * QUAD * D : (q + 1) * QUAD * D])

        for k in range(2):
            nc.sync.dma_start(
                out=pooled_sb[0][:, k * 4 * A : (k + 1) * 4 * A], in_=pooled_f[:, k * 4 * A : (k + 1) * 4 * A]
            )
        nc.sync.dma_start(out=wabs_raw[:], in_=W_abs)
        nc.sync.dma_start(
            out=wraw[0][:].rearrange("p (u x) -> p u x", u=2),
            in_=W_merge[0:D, :].rearrange("(u p e) c -> p u (e c)", u=2, e=2),
        )
        load_pooled(1)
        load_data(0)
        nc.sync.dma_start(out=wraw[1][:], in_=W_merge[D : 2 * D, :].rearrange("(p j) c -> p (j c)", j=4))
        load_pooled(2)
        for q in range(1, 3):
            load_data(q)
        load_pooled(3)
        for q in range(3, QUADS):
            load_data(q)

        idle = keep.tile([P, D], BF16, name="idle")
        nc.vector.memset(idle[:], 0.0)
        ident_b = keep.tile([P, P], BF16, name="ident_b")
        make_identity(nc, ident_b[:])
        ident_f = keep.tile([P, P], F32, name="ident_f")
        make_identity(nc, ident_f[:])

        def drain(on_vector, dst, src):
            if on_vector:
                nc.vector.tensor_copy(out=dst, in_=src)
            else:
                nc.scalar.copy(out=dst, in_=src)

        gx = {}
        xq = {}

        def grouped(b):
            if b not in gx:
                gx[b] = gx_pool.tile([P, 4 * D], BF16, name="gx%d" % b, tag="gx", align_bytes=64)
            return gx[b]

        def quantise(b):
            codes = xq_pool.tile([P, 4 * P], U32, name="xc%d" % b, tag="xc", align_bytes=64)
            scales = xq_pool.tile([P, 4 * P], U8, name="xs%d" % b, tag="xs", align_bytes=64)
            nc.vector.quantize_mx(out=codes[:].bitcast(FP8X4), scales=scales[:], in_=gx[b][:])
            xq[b] = (codes, scales)

        pT = []
        for g in range(4):
            pT.append(keep.tile([A, 8 * P], BF16, name="pT%d" % g))

        def pooled_T(g, on_vector, first=0, tiles=8):
            bank = ring.tile([P, tiles * P], BF16, name="bp%d_%d" % (g, first), tag="ring")
            for k in range(tiles):
                nc.tensor.transpose(
                    bank[:, k * P : (k + 1) * P], pooled_sb[g][:, (first + k) * A : (first + k + 1) * A], ident_b[:]
                )
            drain(on_vector, pT[g][:, first * P : (first + tiles) * P], bank[:])

        def data_T(b, on_vector):
            q = b // 2
            bank = ring.tile([P, D], F32, name="bd%d" % b, tag="ring")
            words = data_sb[q][:].bitcast(F32)
            for i in range(2):
                for u in range(2):
                    col = ((b % 2) * 2 + i) * (D // 2) + u * P
                    nc.tensor.transpose(
                        bank[:, (2 * i + u) * P : (2 * i + u + 1) * P], words[:, col : col + P], ident_f[:]
                    )
            dst = grouped(b)[:].bitcast(F32)[:, 0:D]
            drain(
                on_vector,
                dst.rearrange("p (i r u) -> p i r u", i=2, u=2),
                bank[:].rearrange("p (i u r) -> p i r u", i=2, u=2),
            )

        warm = [0]

        def warm_up(n):
            bank = ring.tile([P, D], F32, name="bw%d" % warm[0], tag="ring")
            warm[0] += 1
            for k in range(n):
                nc.tensor.matmul(out=bank[:], lhsT=idle[:, 0:P], rhs=idle[:], start=True, stop=True)

        wabs_p = keep.tile([A, D], BF16, name="wabs_p")

        def abstract(b, on_vector):
            bank = ring.tile([P, 4 * PAIR], BF16, name="ba%d" % b, tag="ring")
            for j in range(4):
                nc.tensor.matmul(
                    out=bank[:, j * PAIR : (j + 1) * PAIR],
                    lhsT=wabs_p[:, j * P : (j + 1) * P],
                    rhs=pT[b // 4][:, (b % 4) * PAIR : (b % 4 + 1) * PAIR],
                    start=True,
                    stop=True,
                )
            drain(
                on_vector,
                grouped(b)[:, 2 * D : 4 * D].rearrange("p (r j) -> p r j", j=4),
                bank[:].rearrange("p (j r) -> p r j", j=4),
            )

        wg = keep.tile([P, 8 * D], BF16, name="wg", align_bytes=64)
        wc = keep.tile([P, 2 * D], U32, name="wc", align_bytes=64)
        ws = keep.tile([P, 2 * D], U8, name="ws", align_bytes=64)

        o_pair = {}

        def merge(t, on_vector):
            codes, scales = xq[t // 2]
            bank = ring.tile([P, D], F32, name="bo%d" % t, tag="ring")
            for h in range(2):
                lo = (h * 2 + t % 2) * P
                nc.tensor.matmul_mx(
                    out=bank[:],
                    lhsT=codes[:, lo : lo + P].bitcast(FP8X4),
                    lhsT_scale=scales[:, lo : lo + P],
                    rhs=wc[:, h * D : (h + 1) * D].bitcast(FP8X4),
                    rhs_scale=ws[:, h * D : (h + 1) * D],
                    start=(h == 0),
                    stop=(h == 1),
                )
            if t % 2 == 0:
                o_pair[t // 2] = o_pool.tile([P, 2 * D], F32, name="o%d" % t, tag="o")
            o_sb = o_pair[t // 2]
            drain(on_vector, o_sb[:, (t % 2) * D : (t % 2 + 1) * D], bank[:])
            if t >= LAST:
                nc.sync.dma_start(out=out_f[:, t * D : (t + 1) * D], in_=o_sb[:, (t % 2) * D : (t % 2 + 1) * D])
            elif t % 2 == 1:
                nc.sync.dma_start(out=out_f[:, (t - 1) * D : (t + 1) * D], in_=o_sb[:])

        nc.vector.tensor_copy(
            out=wabs_p[:].rearrange("a (j m) -> a j m", j=4),
            in_=wabs_raw[:].rearrange("a (m j) -> a j m", j=4),
        )

        def group_w(h):
            nc.vector.tensor_copy(
                out=wg[:, h * 4 * D : (h + 1) * 4 * D].rearrange("p (c i t) -> p c t i", i=4, t=4),
                in_=wraw[h][:].rearrange("p (t c i) -> p c t i", t=4, i=4),
            )

        def quantise_w(h):
            nc.vector.quantize_mx(
                out=wc[:, h * D : (h + 1) * D].bitcast(FP8X4),
                scales=ws[:, h * D : (h + 1) * D],
                in_=wg[:, h * 4 * D : (h + 1) * 4 * D],
            )

        warm_up(2)
        pooled_T(0, False, 0, 4)
        pooled_T(0, False, 4, 4)
        group_w(0)
        warm_up(2)
        abstract(0, False)
        pooled_T(1, False)
        abstract(1, True)
        abstract(2, False)
        group_w(1)
        data_T(0, False)
        data_T(1, True)
        abstract(3, False)
        quantise_w(0)
        pooled_T(2, True)
        quantise(0)
        abstract(4, False)
        quantise_w(1)
        data_T(2, True)
        data_T(3, False)
        quantise(1)
        abstract(5, False)
        data_T(4, True)
        data_T(5, False)
        pooled_T(3, True)

        for q in range(QUADS):
            fill = q + 3 - q // 3 if q % 3 != 2 else QUADS
            filling = fill < QUADS
            if filling:
                abstract(2 * fill, False)
                data_T(2 * fill, True)
                data_T(2 * fill + 1, True)
                abstract(2 * fill + 1, False)
            for half in range(2):
                if q + 1 < QUADS:
                    quantise(2 * q + 2 + half)
                merge(QUAD * q + 2 * half, False)
                merge(QUAD * q + 2 * half + 1, True)
